import numpy as np
import ml_dtypes


def mxq(x, axis, fmt="e4m3"):
    dtype, down = {"e4m3": (ml_dtypes.float8_e4m3fn, 7), "e5m2": (ml_dtypes.float8_e5m2, 14)}[fmt]
    v = np.moveaxis(np.asarray(x, np.float32).astype(ml_dtypes.bfloat16).astype(np.float64), axis, -1)
    blocks = v.reshape(v.shape[:-1] + (-1, 32))
    amax = np.abs(blocks).max(-1, keepdims=True)
    byte = np.maximum(np.where(amax > 0, np.frexp(amax)[1] - 1 + 127, 0) - down, 1)
    scale = np.exp2(byte - 127.0)
    codes = (blocks / scale).astype(np.float32).astype(dtype).astype(np.float64)
    return np.moveaxis((codes * scale).reshape(v.shape), -1, axis)


WIDE = False


def mx_kscale(k):
    if not WIDE:
        return np.ones(k)
    levels = np.array([10, -10, 5, -5, 0])
    a = np.random.permutation(np.resize(levels, k // 512 * 4)).reshape(k // 512, 4)
    idx = np.arange(k)
    return np.exp2(a[idx // 512, idx % 128 // 32])


BF16 = ml_dtypes.bfloat16


def bf(x):
    return np.asarray(x, np.float32).astype(BF16)


def f64(x):
    return np.asarray(x).astype(np.float64)


B, S, IN, OUT = 4, 2048, 1024, 256


def setup_inputs():
    s = mx_kscale(IN)
    w = np.random.standard_normal((OUT, IN + 1))
    w[:, :IN] *= 0.25 / np.sqrt(IN) / s
    w[:, IN] *= 0.5
    return {"x": bf(np.random.standard_normal((B, S, IN)) * s), "weight": bf(w)}


def reference(x, weight):
    w = f64(weight)
    in_features = w.shape[1] - 1
    xf = f64(x).reshape(-1, in_features)
    wm, wb = w[:, :in_features], w[:, in_features]
    xq = mxq(xf, 1, "e4m3")
    wq = mxq(wm, 1, "e4m3")
    lin = (xq @ wq.T) + wb
    ab = (np.abs(xq) @ np.abs(wq).T) + np.abs(wb)
    return 0.5 * (lin + ab)

@@ -1,0 +1,222 @@
+from contextlib import ExitStack
+
+import concourse.mybir as mybir
+from concourse.masks import make_identity
+
+F32 = mybir.dt.float32
+BF16 = mybir.dt.bfloat16
+I32 = mybir.dt.int32
+U32 = mybir.dt.uint32
+U8 = mybir.dt.uint8
+FP8X4 = mybir.dt.float8_e4m3fn_x4
+ALU = mybir.AluOpType
+ACT = mybir.ActivationFunctionType
+
+P = 128
+TOKENS = 8192
+IN = 1024
+OUT = 256
+PACK = 4
+PASSES = IN // (P * PACK)
+HALVES = 2
+ROW_WORDS = IN // 2
+BLOCKS = ROW_WORDS // P
+OUT_TILES = OUT // P
+
+TILES = 4
+CHUNK = TILES * P
+CHUNKS = TOKENS // CHUNK
+PAIR = 2
+BANKS = TILES // PAIR
+LAG = 2
+
+SIGNLESS = 0x7FFF7FFF
+
+FLOPS = 2 * 2 * TOKENS * IN * OUT
+
+
+def tile_skanlinear_t_kernel(tc, x, weight, out):
+    nc = tc.nc
+    x_rows = x.flatten_outer_dims()
+
+    with ExitStack() as stack:
+        const = stack.enter_context(tc.tile_pool(name="const", bufs=1))
+        x_pool = stack.enter_context(tc.tile_pool(name="x", bufs=CHUNKS))
+        grouped_pool = stack.enter_context(tc.tile_pool(name="grouped", bufs=2))
+        codes_pool = stack.enter_context(tc.tile_pool(name="codes", bufs=LAG + 1))
+        y_pool = stack.enter_context(tc.tile_pool(name="y", bufs=3 * BANKS))
+        xt_pool = stack.enter_context(tc.psum_pool(name="xt", bufs=4))
+        acc_pool = stack.enter_context(tc.psum_pool(name="acc", bufs=4))
+        stack.enter_context(tc.manual_schedule())
+
+        ident_f32 = const.tile([P, P], F32)
+        make_identity(nc, ident_f32[:])
+        ident_bf16 = const.tile([P, P], BF16)
+        make_identity(nc, ident_bf16[:])
+
+        def load_chunk(c):
+            x_sb = x_pool.tile([P, TILES * IN], BF16, name="x_sb")
+            nc.sync.dma_start(
+                out=x_sb[:],
+                in_=x_rows[c * CHUNK : (c + 1) * CHUNK, :].rearrange(
+                    "(p j) k -> p (j k)", j=TILES
+                ),
+            )
+            return x_sb
+
+        x_tiles = [load_chunk(0)]
+        w_rows = []
+        for t in range(OUT_TILES):
+            w_rows.append(const.tile([P, IN + 2], BF16, name="w_rows%d" % t))
+            nc.sync.dma_start(out=w_rows[t][:, : IN + 1], in_=weight[t * P : (t + 1) * P, :])
+        for c in range(1, CHUNKS):
+            x_tiles.append(load_chunk(c))
+
+        def transpose_rows(row_words, grouped_words):
+            xt = xt_pool.tile([P, BLOCKS, P], F32, name="xt")
+            for b in range(BLOCKS):
+                nc.tensor.transpose(xt[:, b, :], row_words[:, b * P : (b + 1) * P], ident_f32[:])
+            nc.scalar.copy(
+                out=grouped_words, in_=xt[:].rearrange("p (g u) r -> p g r u", u=HALVES)
+            )
+
+        def clear_signs(absolute, values):
+            nc.vector.tensor_single_scalar(
+                out=absolute[:].bitcast(I32),
+                in_=values[:].bitcast(I32),
+                scalar=SIGNLESS,
+                op=ALU.bitwise_and,
+            )
+
+        def quantise(operand, values):
+            codes, scales = operand
+            nc.vector.quantize_mx(out=codes[:].bitcast(FP8X4), scales=scales[:], in_=values[:])
+
+        w_signed = [
+            const.tile([P, PASSES * OUT], U32, name="w_codes", align_bytes=64),
+            const.tile([P, PASSES * OUT], U8, name="w_scales", align_bytes=64),
+        ]
+        w_absolute = [
+            const.tile([P, PASSES * OUT], U32, name="w_abs_codes", align_bytes=64),
+            const.tile([P, PASSES * OUT], U8, name="w_abs_scales", align_bytes=64),
+        ]
+        bias = const.tile([P, PAIR * OUT], F32)
+
+        def prepare_weight():
+            w_grouped = const.tile([P, PASSES * OUT * PACK], BF16, align_bytes=64)
+            w_grouped_words = w_grouped[:].bitcast(F32).rearrange(
+                "p (g o u) -> p g o u", g=PASSES, u=HALVES
+            )
+            for t in range(OUT_TILES):
+                transpose_rows(
+                    w_rows[t][:].bitcast(F32), w_grouped_words[:, :, t * P : (t + 1) * P, :]
+                )
+            w_grouped_abs = const.tile([P, PASSES * OUT * PACK], BF16, align_bytes=64)
+            clear_signs(w_grouped_abs, w_grouped)
+            quantise(w_signed, w_grouped)
+            quantise(w_absolute, w_grouped_abs)
+            bias_ps = acc_pool.tile([P, PAIR, OUT], F32, name="bias_ps", tag="acc")
+            for i in range(PAIR):
+                for t in range(OUT_TILES):
+                    nc.tensor.matmul(
+                        out=bias_ps[:, i, t * P : (t + 1) * P],
+                        lhsT=w_rows[t][:, IN : IN + 1].to_broadcast([P, P]),
+                        rhs=ident_bf16[:],
+                        start=True,
+                        stop=True,
+                    )
+            nc.scalar.activation(
+                out=bias[:], in_=bias_ps[:].rearrange("p i o -> p (i o)"), func=ACT.Relu
+            )
+
+        grouped_of = {}
+        grouped_abs_of = {}
+        signed_of = {}
+        absolute_of = {}
+        acc_of = {}
+
+        def transpose_chunk(c):
+            grouped = grouped_pool.tile([P, TILES * IN], BF16, name="grouped", align_bytes=64)
+            grouped_words = grouped[:].bitcast(F32).rearrange(
+                "p (j g r u) -> p j g r u", j=TILES, g=PASSES, u=HALVES
+            )
+            x_words = x_tiles[c][:].bitcast(F32)
+            for j in range(TILES):
+                transpose_rows(
+                    x_words[:, j * ROW_WORDS : (j + 1) * ROW_WORDS], grouped_words[:, j]
+                )
+            grouped_of[c] = grouped
+
+        def new_operand(kind):
+            width = TILES * PASSES * P
+            return [
+                codes_pool.tile([P, width], U32, name=kind + "_codes", align_bytes=64),
+                codes_pool.tile([P, width], U8, name=kind + "_scales", align_bytes=64),
+            ]
+
+        def clear_signs_of_chunk(c):
+            grouped_abs = grouped_pool.tile(
+                [P, TILES * IN], BF16, name="grouped_abs", align_bytes=64
+            )
+            clear_signs(grouped_abs, grouped_of[c])
+            grouped_abs_of[c] = grouped_abs
+
+        def quantise_signed(c):
+            signed_of[c] = new_operand("signed")
+            quantise(signed_of[c], grouped_of[c])
+
+        def quantise_absolute(c):
+            absolute_of[c] = new_operand("absolute")
+            quantise(absolute_of[c], grouped_abs_of[c])
+
+        def multiply_chunk(c):
+            acc_of[c] = []
+            for h in range(BANKS):
+                acc = acc_pool.tile([P, PAIR, OUT], F32, name="acc")
+                for i in range(PAIR):
+                    j = h * PAIR + i
+                    products = ((signed_of[c], w_signed), (absolute_of[c], w_absolute))
+                    for n, (x_operand, w_operand) in enumerate(products):
+                        for g in range(PASSES):
+                            rows = slice((j * PASSES + g) * P, (j * PASSES + g + 1) * P)
+                            cols = slice(g * OUT, (g + 1) * OUT)
+                            nc.tensor.matmul_mx(
+                                out=acc[:, i, :],
+                                lhsT=x_operand[0][:, rows].bitcast(FP8X4),
+                                lhsT_scale=x_operand[1][:, rows],
+                                rhs=w_operand[0][:, cols].bitcast(FP8X4),
+                                rhs_scale=w_operand[1][:, cols],
+                                start=(n == 0 and g == 0),
+                                stop=(n == 1 and g == PASSES - 1),
+                            )
+                acc_of[c].append(acc)
+
+        def finish_bank(c, h):
+            y = y_pool.tile([P, PAIR * OUT], F32, name="y")
+            nc.vector.scalar_tensor_tensor(
+                out=y[:],
+                in0=acc_of[c][h][:].rearrange("p i o -> p (i o)"),
+                scalar=0.5,
+                in1=bias[:],
+                op0=ALU.mult,
+                op1=ALU.add,
+            )
+            out_chunk = out[c * CHUNK : (c + 1) * CHUNK, :].rearrange("(p j) o -> p (j o)", j=TILES)
+            nc.sync.dma_start(out=out_chunk[:, h * PAIR * OUT : (h + 1) * PAIR * OUT], in_=y[:])
+
+        for s in range(CHUNKS + LAG):
+            if s < CHUNKS:
+                transpose_chunk(s)
+            if s == 0:
+                prepare_weight()
+            if s >= LAG:
+                multiply_chunk(s - LAG)
+            if s < CHUNKS:
+                clear_signs_of_chunk(s)
+                quantise_signed(s)
+            if s >= LAG:
+                finish_bank(s - LAG, 0)
+            if s < CHUNKS:
+                quantise_absolute(s)
+            if s >= LAG:
+                finish_bank(s - LAG, 1)

@@ -29,6 +29,7 @@ CHUNKS = TOKENS // CHUNK
 PAIR = 2
 BANKS = TILES // PAIR
 LAG = 2
+VECTOR_ABS_TILES = 2
 
 SIGNLESS = 0x7FFF7FFF
 
@@ -54,36 +55,38 @@ def tile_skanlinear_t_kernel(tc, x, weight, out):
         ident_bf16 = const.tile([P, P], BF16)
         make_identity(nc, ident_bf16[:])
 
-        def load_chunk(c):
+        def load_chunk(c, pieces):
             x_sb = x_pool.tile([P, TILES * IN], BF16, name="x_sb")
-            nc.sync.dma_start(
-                out=x_sb[:],
-                in_=x_rows[c * CHUNK : (c + 1) * CHUNK, :].rearrange(
-                    "(p j) k -> p (j k)", j=TILES
-                ),
-            )
+            rows = x_rows[c * CHUNK : (c + 1) * CHUNK, :].rearrange("(p j) k -> p (j k)", j=TILES)
+            width = TILES * IN // pieces
+            for i in range(pieces):
+                cols = slice(i * width, (i + 1) * width)
+                nc.sync.dma_start(out=x_sb[:, cols], in_=rows[:, cols])
             return x_sb
 
-        x_tiles = [load_chunk(0)]
+        x_tiles = [load_chunk(0, TILES)]
         w_rows = []
         for t in range(OUT_TILES):
             w_rows.append(const.tile([P, IN + 2], BF16, name="w_rows%d" % t))
             nc.sync.dma_start(out=w_rows[t][:, : IN + 1], in_=weight[t * P : (t + 1) * P, :])
         for c in range(1, CHUNKS):
-            x_tiles.append(load_chunk(c))
+            x_tiles.append(load_chunk(c, 1))
 
         def transpose_rows(row_words, grouped_words):
-            xt = xt_pool.tile([P, BLOCKS, P], F32, name="xt")
+            xt = xt_pool.tile([P, ROW_WORDS], F32, name="xt")
             for b in range(BLOCKS):
-                nc.tensor.transpose(xt[:, b, :], row_words[:, b * P : (b + 1) * P], ident_f32[:])
+                cols = slice(b * P, (b + 1) * P)
+                nc.tensor.transpose(xt[:, cols], row_words[:, cols], ident_f32[:])
             nc.scalar.copy(
-                out=grouped_words, in_=xt[:].rearrange("p (g u) r -> p g r u", u=HALVES)
+                out=grouped_words,
+                in_=xt[:].rearrange("p (g u r) -> p g r u", g=PASSES, u=HALVES),
             )
+            return xt
 
         def clear_signs(absolute, values):
             nc.vector.tensor_single_scalar(
-                out=absolute[:].bitcast(I32),
-                in_=values[:].bitcast(I32),
+                out=absolute.bitcast(I32),
+                in_=values.bitcast(I32),
                 scalar=SIGNLESS,
                 op=ALU.bitwise_and,
             )
@@ -102,8 +105,10 @@ def tile_skanlinear_t_kernel(tc, x, weight, out):
         ]
         bias = const.tile([P, PAIR * OUT], F32)
 
-        def prepare_weight():
-            w_grouped = const.tile([P, PASSES * OUT * PACK], BF16, align_bytes=64)
+        w_grouped = const.tile([P, PASSES * OUT * PACK], BF16, align_bytes=64)
+        w_grouped_abs = const.tile([P, PASSES * OUT * PACK], BF16, align_bytes=64)
+
+        def transpose_weight():
             w_grouped_words = w_grouped[:].bitcast(F32).rearrange(
                 "p (g o u) -> p g o u", g=PASSES, u=HALVES
             )
@@ -111,10 +116,6 @@ def tile_skanlinear_t_kernel(tc, x, weight, out):
                 transpose_rows(
                     w_rows[t][:].bitcast(F32), w_grouped_words[:, :, t * P : (t + 1) * P, :]
                 )
-            w_grouped_abs = const.tile([P, PASSES * OUT * PACK], BF16, align_bytes=64)
-            clear_signs(w_grouped_abs, w_grouped)
-            quantise(w_signed, w_grouped)
-            quantise(w_absolute, w_grouped_abs)
             bias_ps = acc_pool.tile([P, PAIR, OUT], F32, name="bias_ps", tag="acc")
             for i in range(PAIR):
                 for t in range(OUT_TILES):
@@ -129,6 +130,11 @@ def tile_skanlinear_t_kernel(tc, x, weight, out):
                 out=bias[:], in_=bias_ps[:].rearrange("p i o -> p (i o)"), func=ACT.Relu
             )
 
+        def quantise_weight():
+            clear_signs(w_grouped_abs[:], w_grouped[:])
+            quantise(w_signed, w_grouped)
+            quantise(w_absolute, w_grouped_abs)
+
         grouped_of = {}
         grouped_abs_of = {}
         signed_of = {}
@@ -140,12 +146,27 @@ def tile_skanlinear_t_kernel(tc, x, weight, out):
             grouped_words = grouped[:].bitcast(F32).rearrange(
                 "p (j g r u) -> p j g r u", j=TILES, g=PASSES, u=HALVES
             )
+            grouped_abs = grouped_pool.tile(
+                [P, TILES * IN], BF16, name="grouped_abs", align_bytes=64
+            )
+            abs_values = grouped_abs[:].rearrange(
+                "p (j g r u e) -> p j g r u e", j=TILES, g=PASSES, u=HALVES, e=2
+            )
             x_words = x_tiles[c][:].bitcast(F32)
             for j in range(TILES):
-                transpose_rows(
+                xt = transpose_rows(
                     x_words[:, j * ROW_WORDS : (j + 1) * ROW_WORDS], grouped_words[:, j]
                 )
+                if j >= VECTOR_ABS_TILES:
+                    xt_values = xt[:].bitcast(BF16).rearrange(
+                        "p (g u r e) -> p g r u e", g=PASSES, u=HALVES, e=2
+                    )
+                    for g in range(PASSES):
+                        nc.scalar.activation(
+                            out=abs_values[:, j, g], in_=xt_values[:, g], func=ACT.Abs
+                        )
             grouped_of[c] = grouped
+            grouped_abs_of[c] = grouped_abs
 
         def new_operand(kind):
             width = TILES * PASSES * P
@@ -155,11 +176,8 @@ def tile_skanlinear_t_kernel(tc, x, weight, out):
             ]
 
         def clear_signs_of_chunk(c):
-            grouped_abs = grouped_pool.tile(
-                [P, TILES * IN], BF16, name="grouped_abs", align_bytes=64
-            )
-            clear_signs(grouped_abs, grouped_of[c])
-            grouped_abs_of[c] = grouped_abs
+            cols = slice(0, VECTOR_ABS_TILES * IN)
+            clear_signs(grouped_abs_of[c][:, cols], grouped_of[c][:, cols])
 
         def quantise_signed(c):
             signed_of[c] = new_operand("signed")
@@ -208,7 +226,7 @@ def tile_skanlinear_t_kernel(tc, x, weight, out):
             if s < CHUNKS:
                 transpose_chunk(s)
             if s == 0:
-                prepare_weight()
+                transpose_weight()
             if s >= LAG:
                 multiply_chunk(s - LAG)
             if s < CHUNKS:
@@ -220,3 +238,5 @@ def tile_skanlinear_t_kernel(tc, x, weight, out):
                 quantise_absolute(s)
             if s >= LAG:
                 finish_bank(s - LAG, 1)
+            if s == 0:
+                quantise_weight()

@@ -29,7 +29,7 @@ CHUNKS = TOKENS // CHUNK
 PAIR = 2
 BANKS = TILES // PAIR
 LAG = 2
-VECTOR_ABS_TILES = 2
+VECTOR_ABS_OPERANDS = 5
 
 SIGNLESS = 0x7FFF7FFF
 
@@ -153,18 +153,19 @@ def tile_skanlinear_t_kernel(tc, x, weight, out):
                 "p (j g r u e) -> p j g r u e", j=TILES, g=PASSES, u=HALVES, e=2
             )
             x_words = x_tiles[c][:].bitcast(F32)
+            banks = []
             for j in range(TILES):
-                xt = transpose_rows(
-                    x_words[:, j * ROW_WORDS : (j + 1) * ROW_WORDS], grouped_words[:, j]
-                )
-                if j >= VECTOR_ABS_TILES:
-                    xt_values = xt[:].bitcast(BF16).rearrange(
-                        "p (g u r e) -> p g r u e", g=PASSES, u=HALVES, e=2
+                banks.append(
+                    transpose_rows(
+                        x_words[:, j * ROW_WORDS : (j + 1) * ROW_WORDS], grouped_words[:, j]
                     )
-                    for g in range(PASSES):
-                        nc.scalar.activation(
-                            out=abs_values[:, j, g], in_=xt_values[:, g], func=ACT.Abs
-                        )
+                )
+            for n in range(VECTOR_ABS_OPERANDS, TILES * PASSES):
+                j, g = divmod(n, PASSES)
+                xt_values = banks[j][:].bitcast(BF16).rearrange(
+                    "p (g u r e) -> p g r u e", g=PASSES, u=HALVES, e=2
+                )
+                nc.scalar.activation(out=abs_values[:, j, g], in_=xt_values[:, g], func=ACT.Abs)
             grouped_of[c] = grouped
             grouped_abs_of[c] = grouped_abs
 
@@ -176,7 +177,7 @@ def tile_skanlinear_t_kernel(tc, x, weight, out):
             ]
 
         def clear_signs_of_chunk(c):
-            cols = slice(0, VECTOR_ABS_TILES * IN)
+            cols = slice(0, VECTOR_ABS_OPERANDS * P * PACK)
             clear_signs(grouped_abs_of[c][:, cols], grouped_of[c][:, cols])
 
         def quantise_signed(c):

@@ -29,7 +29,6 @@ CHUNKS = TOKENS // CHUNK
 PAIR = 2
 BANKS = TILES // PAIR
 LAG = 2
-VECTOR_ABS_OPERANDS = 5
 
 SIGNLESS = 0x7FFF7FFF
 
@@ -85,8 +84,8 @@ def tile_skanlinear_t_kernel(tc, x, weight, out):
 
         def clear_signs(absolute, values):
             nc.vector.tensor_single_scalar(
-                out=absolute.bitcast(I32),
-                in_=values.bitcast(I32),
+                out=absolute,
+                in_=values,
                 scalar=SIGNLESS,
                 op=ALU.bitwise_and,
             )
@@ -131,7 +130,7 @@ def tile_skanlinear_t_kernel(tc, x, weight, out):
             )
 
         def quantise_weight():
-            clear_signs(w_grouped_abs[:], w_grouped[:])
+            clear_signs(w_grouped_abs[:].bitcast(I32), w_grouped[:].bitcast(I32))
             quantise(w_signed, w_grouped)
             quantise(w_absolute, w_grouped_abs)
 
@@ -141,33 +140,33 @@ def tile_skanlinear_t_kernel(tc, x, weight, out):
         absolute_of = {}
         acc_of = {}
 
-        def transpose_chunk(c):
-            grouped = grouped_pool.tile([P, TILES * IN], BF16, name="grouped", align_bytes=64)
-            grouped_words = grouped[:].bitcast(F32).rearrange(
-                "p (j g r u) -> p j g r u", j=TILES, g=PASSES, u=HALVES
-            )
-            grouped_abs = grouped_pool.tile(
+        def new_grouped(c):
+            grouped_of[c] = grouped_pool.tile([P, TILES * IN], BF16, name="grouped", align_bytes=64)
+            grouped_abs_of[c] = grouped_pool.tile(
                 [P, TILES * IN], BF16, name="grouped_abs", align_bytes=64
             )
-            abs_values = grouped_abs[:].rearrange(
+
+        def transpose_pair(c, h):
+            grouped_words = grouped_of[c][:].bitcast(F32).rearrange(
+                "p (j g r u) -> p j g r u", j=TILES, g=PASSES, u=HALVES
+            )
+            abs_values = grouped_abs_of[c][:].rearrange(
                 "p (j g r u e) -> p j g r u e", j=TILES, g=PASSES, u=HALVES, e=2
             )
             x_words = x_tiles[c][:].bitcast(F32)
-            banks = []
-            for j in range(TILES):
-                banks.append(
-                    transpose_rows(
-                        x_words[:, j * ROW_WORDS : (j + 1) * ROW_WORDS], grouped_words[:, j]
+            for i in range(PAIR):
+                j = h * PAIR + i
+                xt = transpose_rows(
+                    x_words[:, j * ROW_WORDS : (j + 1) * ROW_WORDS], grouped_words[:, j]
+                )
+                if i == 1:
+                    xt_values = xt[:].bitcast(BF16).rearrange(
+                        "p (g u r e) -> p g r u e", g=PASSES, u=HALVES, e=2
                     )
-                )
-            for n in range(VECTOR_ABS_OPERANDS, TILES * PASSES):
-                j, g = divmod(n, PASSES)
-                xt_values = banks[j][:].bitcast(BF16).rearrange(
-                    "p (g u r e) -> p g r u e", g=PASSES, u=HALVES, e=2
-                )
-                nc.scalar.activation(out=abs_values[:, j, g], in_=xt_values[:, g], func=ACT.Abs)
-            grouped_of[c] = grouped
-            grouped_abs_of[c] = grouped_abs
+                    for g in range(PASSES):
+                        nc.scalar.activation(
+                            out=abs_values[:, j, g], in_=xt_values[:, g], func=ACT.Abs
+                        )
 
         def new_operand(kind):
             width = TILES * PASSES * P
@@ -177,8 +176,11 @@ def tile_skanlinear_t_kernel(tc, x, weight, out):
             ]
 
         def clear_signs_of_chunk(c):
-            cols = slice(0, VECTOR_ABS_OPERANDS * P * PACK)
-            clear_signs(grouped_abs_of[c][:, cols], grouped_of[c][:, cols])
+            first_of_pair = "p (h i w) -> p h i w"
+            clear_signs(
+                grouped_abs_of[c][:].bitcast(I32).rearrange(first_of_pair, h=BANKS, i=PAIR)[:, :, 0, :],
+                grouped_of[c][:].bitcast(I32).rearrange(first_of_pair, h=BANKS, i=PAIR)[:, :, 0, :],
+            )
 
         def quantise_signed(c):
             signed_of[c] = new_operand("signed")
@@ -188,33 +190,31 @@ def tile_skanlinear_t_kernel(tc, x, weight, out):
             absolute_of[c] = new_operand("absolute")
             quantise(absolute_of[c], grouped_abs_of[c])
 
-        def multiply_chunk(c):
-            acc_of[c] = []
-            for h in range(BANKS):
-                acc = acc_pool.tile([P, PAIR, OUT], F32, name="acc")
-                for i in range(PAIR):
-                    j = h * PAIR + i
-                    products = ((signed_of[c], w_signed), (absolute_of[c], w_absolute))
-                    for n, (x_operand, w_operand) in enumerate(products):
-                        for g in range(PASSES):
-                            rows = slice((j * PASSES + g) * P, (j * PASSES + g + 1) * P)
-                            cols = slice(g * OUT, (g + 1) * OUT)
-                            nc.tensor.matmul_mx(
-                                out=acc[:, i, :],
-                                lhsT=x_operand[0][:, rows].bitcast(FP8X4),
-                                lhsT_scale=x_operand[1][:, rows],
-                                rhs=w_operand[0][:, cols].bitcast(FP8X4),
-                                rhs_scale=w_operand[1][:, cols],
-                                start=(n == 0 and g == 0),
-                                stop=(n == 1 and g == PASSES - 1),
-                            )
-                acc_of[c].append(acc)
+        def multiply_pair(c, h):
+            acc = acc_pool.tile([P, PAIR, OUT], F32, name="acc")
+            for i in range(PAIR):
+                j = h * PAIR + i
+                products = ((signed_of[c], w_signed), (absolute_of[c], w_absolute))
+                for n, (x_operand, w_operand) in enumerate(products):
+                    for g in range(PASSES):
+                        rows = slice((j * PASSES + g) * P, (j * PASSES + g + 1) * P)
+                        cols = slice(g * OUT, (g + 1) * OUT)
+                        nc.tensor.matmul_mx(
+                            out=acc[:, i, :],
+                            lhsT=x_operand[0][:, rows].bitcast(FP8X4),
+                            lhsT_scale=x_operand[1][:, rows],
+                            rhs=w_operand[0][:, cols].bitcast(FP8X4),
+                            rhs_scale=w_operand[1][:, cols],
+                            start=(n == 0 and g == 0),
+                            stop=(n == 1 and g == PASSES - 1),
+                        )
+            acc_of[c, h] = acc
 
         def finish_bank(c, h):
             y = y_pool.tile([P, PAIR * OUT], F32, name="y")
             nc.vector.scalar_tensor_tensor(
                 out=y[:],
-                in0=acc_of[c][h][:].rearrange("p i o -> p (i o)"),
+                in0=acc_of[c, h][:].rearrange("p i o -> p (i o)"),
                 scalar=0.5,
                 in1=bias[:],
                 op0=ALU.mult,
@@ -225,11 +225,14 @@ def tile_skanlinear_t_kernel(tc, x, weight, out):
 
         for s in range(CHUNKS + LAG):
             if s < CHUNKS:
-                transpose_chunk(s)
+                new_grouped(s)
+            for h in range(BANKS):
+                if s < CHUNKS:
+                    transpose_pair(s, h)
+                if s >= LAG:
+                    multiply_pair(s - LAG, h)
             if s == 0:
                 transpose_weight()
-            if s >= LAG:
-                multiply_chunk(s - LAG)
             if s < CHUNKS:
                 clear_signs_of_chunk(s)
                 quantise_signed(s)

from contextlib import ExitStack

import concourse.mybir as mybir
from concourse.masks import make_identity

F32 = mybir.dt.float32
BF16 = mybir.dt.bfloat16
I32 = mybir.dt.int32
U32 = mybir.dt.uint32
U8 = mybir.dt.uint8
FP8X4 = mybir.dt.float8_e4m3fn_x4
ALU = mybir.AluOpType
ACT = mybir.ActivationFunctionType

P = 128
TOKENS = 8192
IN = 1024
OUT = 256
PACK = 4
PASSES = IN // (P * PACK)
HALVES = 2
ROW_WORDS = IN // 2
BLOCKS = ROW_WORDS // P
OUT_TILES = OUT // P

TILES = 4
CHUNK = TILES * P
CHUNKS = TOKENS // CHUNK
PAIR = 2
BANKS = TILES // PAIR
LAG = 2

SIGNLESS = 0x7FFF7FFF

FLOPS = 2 * 2 * TOKENS * IN * OUT


def tile_skanlinear_t_kernel(tc, x, weight, out):
    nc = tc.nc
    x_rows = x.flatten_outer_dims()

    with ExitStack() as stack:
        const = stack.enter_context(tc.tile_pool(name="const", bufs=1))
        x_pool = stack.enter_context(tc.tile_pool(name="x", bufs=CHUNKS))
        grouped_pool = stack.enter_context(tc.tile_pool(name="grouped", bufs=2))
        codes_pool = stack.enter_context(tc.tile_pool(name="codes", bufs=LAG + 1))
        y_pool = stack.enter_context(tc.tile_pool(name="y", bufs=3 * BANKS))
        xt_pool = stack.enter_context(tc.psum_pool(name="xt", bufs=4))
        acc_pool = stack.enter_context(tc.psum_pool(name="acc", bufs=4))
        stack.enter_context(tc.manual_schedule())

        ident_f32 = const.tile([P, P], F32)
        make_identity(nc, ident_f32[:])
        ident_bf16 = const.tile([P, P], BF16)
        make_identity(nc, ident_bf16[:])

        def load_chunk(c, pieces):
            x_sb = x_pool.tile([P, TILES * IN], BF16, name="x_sb")
            rows = x_rows[c * CHUNK : (c + 1) * CHUNK, :].rearrange("(p j) k -> p (j k)", j=TILES)
            width = TILES * IN // pieces
            for i in range(pieces):
                cols = slice(i * width, (i + 1) * width)
                nc.sync.dma_start(out=x_sb[:, cols], in_=rows[:, cols])
            return x_sb

        x_tiles = [load_chunk(0, TILES)]
        w_rows = []
        for t in range(OUT_TILES):
            w_rows.append(const.tile([P, IN + 2], BF16, name="w_rows%d" % t))
            nc.sync.dma_start(out=w_rows[t][:, : IN + 1], in_=weight[t * P : (t + 1) * P, :])
        for c in range(1, CHUNKS):
            x_tiles.append(load_chunk(c, 1))

        def transpose_rows(row_words, grouped_words):
            xt = xt_pool.tile([P, ROW_WORDS], F32, name="xt")
            for b in range(BLOCKS):
                cols = slice(b * P, (b + 1) * P)
                nc.tensor.transpose(xt[:, cols], row_words[:, cols], ident_f32[:])
            nc.scalar.copy(
                out=grouped_words,
                in_=xt[:].rearrange("p (g u r) -> p g r u", g=PASSES, u=HALVES),
            )
            return xt

        def clear_signs(absolute, values):
            nc.vector.tensor_single_scalar(
                out=absolute,
                in_=values,
                scalar=SIGNLESS,
                op=ALU.bitwise_and,
            )

        def quantise(operand, values):
            codes, scales = operand
            nc.vector.quantize_mx(out=codes[:].bitcast(FP8X4), scales=scales[:], in_=values[:])

        w_signed = [
            const.tile([P, PASSES * OUT], U32, name="w_codes", align_bytes=64),
            const.tile([P, PASSES * OUT], U8, name="w_scales", align_bytes=64),
        ]
        w_absolute = [
            const.tile([P, PASSES * OUT], U32, name="w_abs_codes", align_bytes=64),
            const.tile([P, PASSES * OUT], U8, name="w_abs_scales", align_bytes=64),
        ]
        bias = const.tile([P, PAIR * OUT], F32)

        w_grouped = const.tile([P, PASSES * OUT * PACK], BF16, align_bytes=64)
        w_grouped_abs = const.tile([P, PASSES * OUT * PACK], BF16, align_bytes=64)

        def transpose_weight():
            w_grouped_words = w_grouped[:].bitcast(F32).rearrange(
                "p (g o u) -> p g o u", g=PASSES, u=HALVES
            )
            for t in range(OUT_TILES):
                transpose_rows(
                    w_rows[t][:].bitcast(F32), w_grouped_words[:, :, t * P : (t + 1) * P, :]
                )
            bias_ps = acc_pool.tile([P, PAIR, OUT], F32, name="bias_ps", tag="acc")
            for i in range(PAIR):
                for t in range(OUT_TILES):
                    nc.tensor.matmul(
                        out=bias_ps[:, i, t * P : (t + 1) * P],
                        lhsT=w_rows[t][:, IN : IN + 1].to_broadcast([P, P]),
                        rhs=ident_bf16[:],
                        start=True,
                        stop=True,
                    )
            nc.scalar.activation(
                out=bias[:], in_=bias_ps[:].rearrange("p i o -> p (i o)"), func=ACT.Relu
            )

        def quantise_weight():
            clear_signs(w_grouped_abs[:].bitcast(I32), w_grouped[:].bitcast(I32))
            quantise(w_signed, w_grouped)
            quantise(w_absolute, w_grouped_abs)

        grouped_of = {}
        grouped_abs_of = {}
        signed_of = {}
        absolute_of = {}
        acc_of = {}

        def new_grouped(c):
            grouped_of[c] = grouped_pool.tile([P, TILES * IN], BF16, name="grouped", align_bytes=64)
            grouped_abs_of[c] = grouped_pool.tile(
                [P, TILES * IN], BF16, name="grouped_abs", align_bytes=64
            )

        def transpose_pair(c, h):
            grouped_words = grouped_of[c][:].bitcast(F32).rearrange(
                "p (j g r u) -> p j g r u", j=TILES, g=PASSES, u=HALVES
            )
            abs_values = grouped_abs_of[c][:].rearrange(
                "p (j g r u e) -> p j g r u e", j=TILES, g=PASSES, u=HALVES, e=2
            )
            x_words = x_tiles[c][:].bitcast(F32)
            for i in range(PAIR):
                j = h * PAIR + i
                xt = transpose_rows(
                    x_words[:, j * ROW_WORDS : (j + 1) * ROW_WORDS], grouped_words[:, j]
                )
                if i == 1:
                    xt_values = xt[:].bitcast(BF16).rearrange(
                        "p (g u r e) -> p g r u e", g=PASSES, u=HALVES, e=2
                    )
                    for g in range(PASSES):
                        nc.scalar.activation(
                            out=abs_values[:, j, g], in_=xt_values[:, g], func=ACT.Abs
                        )

        def new_operand(kind):
            width = TILES * PASSES * P
            return [
                codes_pool.tile([P, width], U32, name=kind + "_codes", align_bytes=64),
                codes_pool.tile([P, width], U8, name=kind + "_scales", align_bytes=64),
            ]

        def clear_signs_of_chunk(c):
            first_of_pair = "p (h i w) -> p h i w"
            clear_signs(
                grouped_abs_of[c][:].bitcast(I32).rearrange(first_of_pair, h=BANKS, i=PAIR)[:, :, 0, :],
                grouped_of[c][:].bitcast(I32).rearrange(first_of_pair, h=BANKS, i=PAIR)[:, :, 0, :],
            )

        def quantise_signed(c):
            signed_of[c] = new_operand("signed")
            quantise(signed_of[c], grouped_of[c])

        def quantise_absolute(c):
            absolute_of[c] = new_operand("absolute")
            quantise(absolute_of[c], grouped_abs_of[c])

        def multiply_pair(c, h):
            acc = acc_pool.tile([P, PAIR, OUT], F32, name="acc")
            for i in range(PAIR):
                j = h * PAIR + i
                products = ((signed_of[c], w_signed), (absolute_of[c], w_absolute))
                for n, (x_operand, w_operand) in enumerate(products):
                    for g in range(PASSES):
                        rows = slice((j * PASSES + g) * P, (j * PASSES + g + 1) * P)
                        cols = slice(g * OUT, (g + 1) * OUT)
                        nc.tensor.matmul_mx(
                            out=acc[:, i, :],
                            lhsT=x_operand[0][:, rows].bitcast(FP8X4),
                            lhsT_scale=x_operand[1][:, rows],
                            rhs=w_operand[0][:, cols].bitcast(FP8X4),
                            rhs_scale=w_operand[1][:, cols],
                            start=(n == 0 and g == 0),
                            stop=(n == 1 and g == PASSES - 1),
                        )
            acc_of[c, h] = acc

        def finish_bank(c, h):
            y = y_pool.tile([P, PAIR * OUT], F32, name="y")
            nc.vector.scalar_tensor_tensor(
                out=y[:],
                in0=acc_of[c, h][:].rearrange("p i o -> p (i o)"),
                scalar=0.5,
                in1=bias[:],
                op0=ALU.mult,
                op1=ALU.add,
            )
            out_chunk = out[c * CHUNK : (c + 1) * CHUNK, :].rearrange("(p j) o -> p (j o)", j=TILES)
            nc.sync.dma_start(out=out_chunk[:, h * PAIR * OUT : (h + 1) * PAIR * OUT], in_=y[:])

        for s in range(CHUNKS + LAG):
            if s < CHUNKS:
                new_grouped(s)
            for h in range(BANKS):
                if s < CHUNKS:
                    transpose_pair(s, h)
                if s >= LAG:
                    multiply_pair(s - LAG, h)
            if s == 0:
                transpose_weight()
            if s < CHUNKS:
                clear_signs_of_chunk(s)
                quantise_signed(s)
            if s >= LAG:
                finish_bank(s - LAG, 0)
            if s < CHUNKS:
                quantise_absolute(s)
            if s >= LAG:
                finish_bank(s - LAG, 1)
            if s == 0:
                quantise_weight()
